import numpy as np
import ml_dtypes


def mxq(x, axis, fmt="e4m3"):
    dtype, down = {"e4m3": (ml_dtypes.float8_e4m3fn, 7), "e5m2": (ml_dtypes.float8_e5m2, 14)}[fmt]
    v = np.moveaxis(np.asarray(x, np.float32).astype(ml_dtypes.bfloat16).astype(np.float64), axis, -1)
    blocks = v.reshape(v.shape[:-1] + (-1, 32))
    amax = np.abs(blocks).max(-1, keepdims=True)
    byte = np.maximum(np.where(amax > 0, np.frexp(amax)[1] - 1 + 127, 0) - down, 1)
    scale = np.exp2(byte - 127.0)
    codes = (blocks / scale).astype(np.float32).astype(dtype).astype(np.float64)
    return np.moveaxis((codes * scale).reshape(v.shape), -1, axis)


WIDE = False


def mx_kscale(k):
    if not WIDE:
        return np.ones(k)
    levels = np.array([10, -10, 5, -5, 0])
    if k % 512:
        return np.exp2(np.random.permutation(np.resize(levels, k // 32))).repeat(32)
    a = np.empty((k // 512, 16))
    for p in range(k // 512):
        a[p, :8] = np.random.permutation(np.resize(levels, 8))
        for g in range(8):
            far = levels[np.abs(levels - a[p, g]) >= 10]
            a[p, g + 8] = far[np.random.randint(len(far))]
    return np.exp2(a.ravel()).repeat(32)


BF16 = ml_dtypes.bfloat16


def bf(x):
    return np.asarray(x, np.float32).astype(BF16)


def f64(x):
    return np.asarray(x).astype(np.float64)


B, N, W, H, A = 4, 256, 2048, 16, 128
HD = H * A


def make_sin_cos():
    lin = np.linspace(0.0, 1.0, A // 2)
    freqs = 10000.0 ** (-np.repeat(lin, 2))
    theta = np.arange(N, dtype=np.float64)[:, None] * freqs[None, :]
    return np.sin(theta), np.cos(theta)


def apply_rope(y, sin, cos):
    yp = y.reshape(y.shape[:-1] + (A // 2, 2))
    yr = np.stack([-yp[..., 1], yp[..., 0]], axis=-1).reshape(y.shape)
    return y * cos + yr * sin


def setup_inputs():
    s = mx_kscale(W)
    return {"x": bf(np.random.standard_normal((B, N, W)) * s),
            "w": bf(np.random.standard_normal((HD, W)) / np.sqrt(W) / s[None, :])}


def core(x, w):
    y = mxq(f64(x), 2, "e4m3") @ mxq(f64(w), 1, "e4m3").T
    y = y.reshape(B, N, H, A).transpose(0, 2, 1, 3)
    sin, cos = make_sin_cos()
    return apply_rope(y, sin, cos)


def e4m3fn_bytes(y):
    return np.clip(np.asarray(y, np.float64), -448.0, 448.0).astype(np.float32).astype(ml_dtypes.float8_e4m3fn).view(np.uint8)


def reference(x, w):
    out = core(x, w)
    s = np.max(np.abs(out), axis=-1, keepdims=True) / 448.0
    return out, e4m3fn_bytes(out / s)

@@ -1,0 +1,332 @@
+import math
+from contextlib import ExitStack
+
+import concourse.masks as masks
+import concourse.mybir as mybir
+
+F32 = mybir.dt.float32
+BF16 = mybir.dt.bfloat16
+I32 = mybir.dt.int32
+U32 = mybir.dt.uint32
+U8 = mybir.dt.uint8
+FP8 = mybir.dt.float8_e4m3fn
+FP8X4 = mybir.dt.float8_e4m3fn_x4
+ALU = mybir.AluOpType
+ACT = mybir.ActivationFunctionType
+AX = mybir.AxisListType
+
+B, N, W, H, A = 4, 256, 2048, 16, 128
+FLOPS = 2 * B * N * W * H * A
+P = 128
+PASSES = W // (4 * P)
+BANK = 512
+PAIRS = A // 2
+PASS_WORDS = 2 * P
+UNIT_HEADS = 2 * A
+STEP_COLUMNS = 2 * W
+STEP_WORDS = STEP_COLUMNS // 4
+FP8_MAX = 448.0
+
+TWO_PI = 2.0 * math.pi
+TWO_PI_HIGH = 6.28125
+TWO_PI_LOW = TWO_PI - TWO_PI_HIGH
+RATIO = 10000.0 ** (-1.0 / (PAIRS - 1))
+
+STEPS = [("W", 0), ("X", 0), ("X", 1), ("W", 1), ("X", 2), ("W", 2), ("X", 3), ("W", 3),
+         ("W", 4), ("W", 5), ("W", 6), ("W", 7)]
+STEPS_IN_HALVES = 2
+
+PRODUCT_LAG = 1
+ADD_LAG = 2
+ROW_MAX_LAG = 3
+RECIPROCAL_LAG = 4
+FACTOR_LAG = 5
+CAST_LAG = 6
+
+
+def build_tables(nc, const, cos_t, sin_t):
+    pos = const.tile([P, 2], F32)
+    nc.gpsimd.iota(pos[:], pattern=[[1, 2]], base=0, channel_multiplier=2,
+                   allow_small_or_imprecise_dtypes=True)
+    freq = const.tile([P, PAIRS], F32)
+    nc.vector.memset(freq[:, 0:1], 1.0)
+    n = 1
+    while n < PAIRS:
+        nc.vector.tensor_scalar(out=freq[:, n:2 * n], in0=freq[:, 0:n], scalar1=RATIO ** n,
+                                scalar2=None, op0=ALU.mult)
+        n *= 2
+    theta = const.tile([P, 2, PAIRS], F32)
+    for s in range(2):
+        nc.vector.tensor_scalar(out=theta[:, s, :], in0=freq[:], scalar1=pos[:, s:s + 1],
+                                scalar2=None, op0=ALU.mult)
+    turns = const.tile([P, 2, PAIRS], F32)
+    nc.vector.tensor_scalar(out=turns[:], in0=theta[:], scalar1=1.0 / TWO_PI, scalar2=None,
+                            op0=ALU.mult)
+    turns_i = const.tile([P, 2, PAIRS], I32)
+    nc.vector.tensor_copy(out=turns_i[:], in_=turns[:])
+    turns_f = const.tile([P, 2, PAIRS], F32)
+    nc.vector.tensor_copy(out=turns_f[:], in_=turns_i[:])
+    red1 = const.tile([P, 2, PAIRS], F32)
+    nc.vector.scalar_tensor_tensor(out=red1[:], in0=turns_f[:], scalar=-TWO_PI_HIGH, in1=theta[:],
+                                   op0=ALU.mult, op1=ALU.add)
+    red2 = const.tile([P, 2, PAIRS], F32)
+    nc.vector.scalar_tensor_tensor(out=red2[:], in0=turns_f[:], scalar=-TWO_PI_LOW, in1=red1[:],
+                                   op0=ALU.mult, op1=ALU.add)
+    wrap_s = const.tile([P, 2, PAIRS], F32)
+    nc.vector.tensor_scalar(out=wrap_s[:], in0=red2[:], scalar1=math.pi, scalar2=-TWO_PI,
+                            op0=ALU.is_gt, op1=ALU.mult)
+    ang_s = const.tile([P, 2, PAIRS], F32)
+    nc.vector.tensor_tensor(out=ang_s[:], in0=red2[:], in1=wrap_s[:], op=ALU.add)
+    shift = const.tile([P, 2, PAIRS], F32)
+    nc.vector.tensor_scalar(out=shift[:], in0=ang_s[:], scalar1=0.5 * math.pi, scalar2=None,
+                            op0=ALU.add)
+    wrap_c = const.tile([P, 2, PAIRS], F32)
+    nc.vector.tensor_scalar(out=wrap_c[:], in0=shift[:], scalar1=math.pi, scalar2=-TWO_PI,
+                            op0=ALU.is_gt, op1=ALU.mult)
+    ang_c = const.tile([P, 2, PAIRS], F32)
+    nc.vector.tensor_tensor(out=ang_c[:], in0=shift[:], in1=wrap_c[:], op=ALU.add)
+
+    cos_b = const.tile([P, 2, PAIRS, 2], F32)
+    sin_b = const.tile([P, 2, PAIRS, 2], F32)
+    nc.scalar.activation(out=sin_b[:, :, :, 0], in_=ang_s[:], func=ACT.Sin, scale=-1.0)
+    nc.scalar.activation(out=sin_b[:, :, :, 1], in_=ang_s[:], func=ACT.Sin, scale=1.0)
+    nc.scalar.activation(out=cos_b[:, :, :, 0], in_=ang_c[:], func=ACT.Sin, scale=1.0)
+    nc.scalar.activation(out=cos_b[:, :, :, 1], in_=ang_c[:], func=ACT.Sin, scale=1.0)
+    for hl in range(2):
+        nc.vector.tensor_copy(out=cos_t[:, :, hl, :], in_=cos_b[:].rearrange("p s f e -> p s (f e)"))
+        nc.vector.tensor_copy(out=sin_t[:, :, hl, :], in_=sin_b[:].rearrange("p s f e -> p s (f e)"))
+
+
+def pairs(ap):
+    return ap.rearrange("p (f e) -> p f e", e=2)
+
+
+def swapped(ap):
+    return pairs(ap)[:, :, ::-1]
+
+
+def head_major(ap):
+    return ap.rearrange("p (s h a) -> p h s a", s=2, h=2)
+
+
+def tile_mha_pa_kernel(tc, x, w, out_0, out_1):
+    nc = tc.nc
+    with ExitStack() as ctx:
+        const = ctx.enter_context(tc.tile_pool(name="const", bufs=1))
+        rawp = ctx.enter_context(tc.tile_pool(name="raw", bufs=16))
+        grpp = ctx.enter_context(tc.tile_pool(name="grp", bufs=3))
+        keep = ctx.enter_context(tc.tile_pool(name="keep", bufs=1))
+        work = ctx.enter_context(tc.tile_pool(name="work", bufs=6))
+        outp = ctx.enter_context(tc.tile_pool(name="outp", bufs=9))
+        tpp = ctx.enter_context(tc.psum_pool(name="tpp", bufs=4))
+        accp = ctx.enter_context(tc.psum_pool(name="accp", bufs=4))
+
+        raws = []
+        for kind, which in STEPS:
+            tiles = []
+            for j in range(2):
+                raw = rawp.tile([P, W], BF16, tag="raw")
+                if kind == "X":
+                    src = x[which].rearrange("(p s) k -> p s k", s=2)[:, j, :]
+                else:
+                    src = w[(2 * which + j) * P:(2 * which + j + 1) * P, :]
+                pieces = 2 if len(raws) < STEPS_IN_HALVES else 1
+                wide = W // pieces
+                for piece in range(pieces):
+                    nc.sync.dma_start(out=raw[:, piece * wide:(piece + 1) * wide],
+                                      in_=src[:, piece * wide:(piece + 1) * wide])
+                tiles.append(raw)
+            raws.append(tiles)
+
+        zeros = const.tile([P, 1], F32)
+        nc.vector.memset(zeros[:], 0.0)
+        warm = const.tile([P, 1], F32)
+        nc.scalar.activation(out=warm[:], in_=zeros[:], func=ACT.Sin)
+        ident = const.tile([P, P], F32)
+        masks.make_identity(nc, ident[:])
+        cos_t = const.tile([P, 2, 2, A], F32)
+        sin_t = const.tile([P, 2, 2, A], F32)
+        build_tables(nc, const, cos_t, sin_t)
+        cos_f = cos_t[:].rearrange("p s h a -> p (s h a)")
+        sin_f = sin_t[:].rearrange("p s h a -> p (s h a)")
+
+        interleaved = {}
+        codes = {}
+        scales = {}
+
+        def turn(step):
+            kind = STEPS[step][0]
+            grp = grpp.tile([P, STEP_COLUMNS], BF16, tag="grp", align_bytes=64)
+            interleaved[step] = grp
+            gw = grp[:].bitcast(F32)
+            if kind == "X":
+                view = gw.rearrange("p (j g r u) -> p j g r u", j=2, g=PASSES, u=2)
+            else:
+                view = gw.rearrange("p (g j r u) -> p j g r u", g=PASSES, j=2, u=2)
+            for half in range(2):
+                for other in range(2):
+                    j, gp = (half, other) if kind == "X" else (other, half)
+                    words = raws[step][j][:].bitcast(F32)
+                    tp = tpp.tile([P, 2, 2, P], F32, tag="tp")
+                    for gg in range(2):
+                        g = 2 * gp + gg
+                        for u in range(2):
+                            nc.tensor.transpose(out=tp[:, gg, u, :],
+                                                in_=words[:, PASS_WORDS * g + u:PASS_WORDS * (g + 1):2],
+                                                identity=ident[:])
+                    nc.scalar.copy(out=view[:, j, 2 * gp:2 * gp + 2, :, :],
+                                   in_=tp[:].rearrange("p g u r -> p g r u"))
+
+        def quant(step):
+            cod = keep.tile([P, STEP_WORDS], U32, tag="cod%d" % step, align_bytes=64)
+            scl = keep.tile([P, STEP_WORDS], U8, tag="scl%d" % step, align_bytes=64)
+            codes[STEPS[step]] = cod
+            scales[STEPS[step]] = scl
+            parts = 2 if step < STEPS_IN_HALVES else 1
+            span = STEP_WORDS // parts
+            for part in range(parts):
+                nc.vector.quantize_mx(out=cod[:, span * part:span * (part + 1)].bitcast(FP8X4),
+                                      scales=scl[:, span * part:span * (part + 1)],
+                                      in_=interleaved[step][:, 4 * span * part:4 * span * (part + 1)])
+
+        units = []
+        first_of = []
+        have = {"X": [], "W": []}
+        for kind, which in STEPS:
+            first_of.append(len(units))
+            if kind == "X":
+                units.extend([(which, c) for c in have["W"]])
+            else:
+                units.extend([(b, which) for b in have["X"]])
+            have[kind].append(which)
+        first_of.append(len(units))
+        n_units = len(units)
+
+        couples = [[2 * m, 2 * m + 1] for m in range(n_units // 2 - 1)] + [[n_units - 2], [n_units - 1]]
+        couple_of = {}
+        recip_slot = {}
+        factor_slot = {}
+        cast_slot = {}
+        for m, members in enumerate(couples):
+            recip_slot[members[-1] + RECIPROCAL_LAG] = m
+            factor_slot[members[-1] + FACTOR_LAG] = m
+            for i in members:
+                couple_of[i] = m
+        at_slot = 0
+        for i in range(n_units):
+            at_slot = max(at_slot + 1, couples[couple_of[i]][-1] + CAST_LAG)
+            cast_slot[at_slot] = i
+        n_slots = at_slot + 1
+
+        accs = {}
+        prods = {}
+        results = {}
+        maxima = {}
+        inverses = {}
+        factors = {}
+
+        def multiply(i):
+            b, c = units[i]
+            xc, xs = codes[("X", b)], scales[("X", b)]
+            wc, ws = codes[("W", c)], scales[("W", c)]
+            acc = accp.tile([P, BANK], F32, tag="acc")
+            for s in range(2):
+                for g in range(PASSES):
+                    xo = (PASSES * s + g) * P
+                    wo = g * UNIT_HEADS
+                    nc.tensor.matmul_mx(out=acc[:, UNIT_HEADS * s:UNIT_HEADS * (s + 1)],
+                                        lhsT=xc[:, xo:xo + P].bitcast(FP8X4),
+                                        lhsT_scale=xs[:, xo:xo + P],
+                                        rhs=wc[:, wo:wo + UNIT_HEADS].bitcast(FP8X4),
+                                        rhs_scale=ws[:, wo:wo + UNIT_HEADS],
+                                        start=(g == 0), stop=(g == PASSES - 1))
+            accs[i] = acc
+
+        def product_cos(i):
+            t1 = work.tile([P, BANK], F32, tag="t1")
+            t2 = work.tile([P, BANK], F32, tag="t2")
+            prods[i] = (t1, t2)
+            nc.vector.tensor_tensor(out=t1[:], in0=accs[i][:], in1=cos_f, op=ALU.mult)
+
+        def product_sin(i):
+            nc.vector.tensor_tensor(out=pairs(prods[i][1][:]), in0=swapped(accs[i][:]),
+                                    in1=pairs(sin_f), op=ALU.mult)
+
+        def combine(i):
+            t1, t2 = prods[i]
+            osb = outp.tile([P, 2, 2, A], F32, tag="osb")
+            nc.gpsimd.tensor_tensor(out=osb[:], in0=head_major(t1[:]), in1=head_major(t2[:]), op=ALU.add)
+            results[i] = osb
+
+        def row_max(i):
+            b, c = units[i]
+            osb = results[i]
+            nc.sync.dma_start(out=out_0[b, 2 * c:2 * c + 2].rearrange("h (p s) a -> p h (s a)", s=2),
+                              in_=osb[:].rearrange("p h s a -> p h (s a)"))
+            m = couple_of[i]
+            if i == couples[m][0]:
+                amax = outp.tile([P, 4 * len(couples[m])], F32, tag="amax")
+                maxima[m] = amax
+            at = 4 * (i - couples[m][0])
+            nc.vector.tensor_reduce(out=maxima[m][:, at:at + 4],
+                                    in_=osb[:].rearrange("p h s a -> p (h s) a"),
+                                    axis=AX.X, op=ALU.max, apply_absolute_value=True)
+
+        def reciprocals(m):
+            rinv = outp.tile([P, 4 * len(couples[m])], F32, tag="rinv")
+            nc.vector.reciprocal(out=rinv[:], in_=maxima[m][:])
+            inverses[m] = rinv
+
+        def row_factors(m):
+            fac = outp.tile([P, 4 * len(couples[m])], F32, tag="fac")
+            nc.scalar.activation(out=fac[:], in_=inverses[m][:], func=ACT.Copy, scale=FP8_MAX)
+            factors[m] = fac
+
+        def cast_rows(i):
+            b, c = units[i]
+            osb = results[i]
+            m = couple_of[i]
+            fac = factors[m]
+            at = 4 * (i - couples[m][0])
+            o8 = outp.tile([P, 2, 2, A], FP8, tag="o8")
+            for hl in range(2):
+                for s in range(2):
+                    col = at + 2 * hl + s
+                    nc.scalar.activation(out=o8[:, hl, s, :], in_=osb[:, hl, s, :], func=ACT.Identity,
+                                         scale=fac[:, col:col + 1], bias=zeros[:, 0:1], saturate=False)
+            nc.sync.dma_start(out=out_1[b, 2 * c:2 * c + 2].rearrange("h (p s) a -> p h (s a)", s=2),
+                              in_=o8[:].bitcast(U8).rearrange("p h s a -> p h (s a)"))
+
+        def slot(i, quantize_step):
+            if i < n_units:
+                multiply(i)
+            if 0 <= i - PRODUCT_LAG < n_units:
+                product_cos(i - PRODUCT_LAG)
+            if i in recip_slot:
+                reciprocals(recip_slot[i])
+            if 0 <= i - PRODUCT_LAG < n_units:
+                product_sin(i - PRODUCT_LAG)
+            if quantize_step is not None:
+                quant(quantize_step)
+            if 0 <= i - ROW_MAX_LAG < n_units:
+                row_max(i - ROW_MAX_LAG)
+            if i in cast_slot:
+                cast_rows(cast_slot[i])
+            if i in factor_slot:
+                row_factors(factor_slot[i])
+            if 0 <= i - ADD_LAG < n_units:
+                combine(i - ADD_LAG)
+
+        with tc.manual_schedule():
+            turn(0)
+            quant(0)
+            turn(1)
+            quant(1)
+            for step in range(1, len(STEPS)):
+                more = step + 1 < len(STEPS)
+                if more:
+                    turn(step + 1)
+                for i in range(first_of[step], first_of[step + 1]):
+                    slot(i, step + 1 if more and i == min(first_of[step] + 1, first_of[step + 1] - 1) else None)
+            for i in range(n_units, n_slots):
+                slot(i, None)

@@ -88,8 +88,8 @@ def build_tables(nc, const, cos_t, sin_t):
 
     cos_b = const.tile([P, 2, PAIRS, 2], F32)
     sin_b = const.tile([P, 2, PAIRS, 2], F32)
-    nc.scalar.activation(out=sin_b[:, :, :, 0], in_=ang_s[:], func=ACT.Sin, scale=-1.0)
-    nc.scalar.activation(out=sin_b[:, :, :, 1], in_=ang_s[:], func=ACT.Sin, scale=1.0)
+    nc.scalar.activation(out=sin_b[:, :, :, 0], in_=ang_s[:], func=ACT.Sin, scale=1.0)
+    nc.scalar.activation(out=sin_b[:, :, :, 1], in_=ang_s[:], func=ACT.Sin, scale=-1.0)
     nc.scalar.activation(out=cos_b[:, :, :, 0], in_=ang_c[:], func=ACT.Sin, scale=1.0)
     nc.scalar.activation(out=cos_b[:, :, :, 1], in_=ang_c[:], func=ACT.Sin, scale=1.0)
     for hl in range(2):
@@ -105,8 +105,12 @@ def swapped(ap):
     return pairs(ap)[:, :, ::-1]
 
 
-def head_major(ap):
-    return ap.rearrange("p (s h a) -> p h s a", s=2, h=2)
+def split(ap):
+    return ap.rearrange("p (s h a) -> p s h a", s=2, h=2)
+
+
+def by_position(ap):
+    return ap.rearrange("p (h s a) -> p s h a", s=2, h=2)
 
 
 def tile_mha_pa_kernel(tc, x, w, out_0, out_1):
@@ -246,16 +250,17 @@ def tile_mha_pa_kernel(tc, x, w, out_0, out_1):
             t1 = work.tile([P, BANK], F32, tag="t1")
             t2 = work.tile([P, BANK], F32, tag="t2")
             prods[i] = (t1, t2)
-            nc.vector.tensor_tensor(out=t1[:], in0=accs[i][:], in1=cos_f, op=ALU.mult)
+            nc.vector.tensor_tensor(out=by_position(t1[:]),
+                                    in0=split(accs[i][:]), in1=split(cos_f), op=ALU.mult)
 
         def product_sin(i):
-            nc.vector.tensor_tensor(out=pairs(prods[i][1][:]), in0=swapped(accs[i][:]),
-                                    in1=pairs(sin_f), op=ALU.mult)
+            nc.vector.tensor_tensor(out=by_position(prods[i][1][:]), in0=split(accs[i][:]), in1=split(sin_f), op=ALU.mult)
 
         def combine(i):
             t1, t2 = prods[i]
             osb = outp.tile([P, 2, 2, A], F32, tag="osb")
-            nc.gpsimd.tensor_tensor(out=osb[:], in0=head_major(t1[:]), in1=head_major(t2[:]), op=ALU.add)
+            nc.gpsimd.tensor_tensor(out=pairs(osb[:].rearrange("p h s a -> p (h s a)")), in0=pairs(t1[:]), in1=swapped(t2[:]),
+                                    op=ALU.add)
             results[i] = osb
 
         def row_max(i):

@@ -34,7 +34,7 @@ RATIO = 10000.0 ** (-1.0 / (PAIRS - 1))
 
 STEPS = [("W", 0), ("X", 0), ("X", 1), ("W", 1), ("X", 2), ("W", 2), ("X", 3), ("W", 3),
          ("W", 4), ("W", 5), ("W", 6), ("W", 7)]
-STEPS_IN_HALVES = 2
+STEPS_IN_HALVES = 4
 
 PRODUCT_LAG = 1
 ADD_LAG = 2
@@ -42,6 +42,12 @@ ROW_MAX_LAG = 3
 RECIPROCAL_LAG = 4
 FACTOR_LAG = 5
 CAST_LAG = 6
+ALONE = 4
+QOFF = 1
+WORK_BUFS = 4
+SUMS_BUFS = 5
+OFFLOAD = ()
+ON_VECTOR = 1
 
 
 def build_tables(nc, const, cos_t, sin_t):
@@ -120,7 +126,9 @@ def tile_mha_pa_kernel(tc, x, w, out_0, out_1):
         rawp = ctx.enter_context(tc.tile_pool(name="raw", bufs=16))
         grpp = ctx.enter_context(tc.tile_pool(name="grp", bufs=3))
         keep = ctx.enter_context(tc.tile_pool(name="keep", bufs=1))
-        work = ctx.enter_context(tc.tile_pool(name="work", bufs=6))
+        work = ctx.enter_context(tc.tile_pool(name="work", bufs=WORK_BUFS))
+        sums = ctx.enter_context(tc.tile_pool(name="sums", bufs=SUMS_BUFS))
+        banks = ctx.enter_context(tc.tile_pool(name="banks", bufs=2))
         outp = ctx.enter_context(tc.tile_pool(name="outp", bufs=9))
         tpp = ctx.enter_context(tc.psum_pool(name="tpp", bufs=4))
         accp = ctx.enter_context(tc.psum_pool(name="accp", bufs=4))
@@ -206,21 +214,29 @@ def tile_mha_pa_kernel(tc, x, w, out_0, out_1):
         first_of.append(len(units))
         n_units = len(units)
 
-        couples = [[2 * m, 2 * m + 1] for m in range(n_units // 2 - 1)] + [[n_units - 2], [n_units - 1]]
+        couples = ([[2 * m, 2 * m + 1] for m in range((n_units - ALONE) // 2)]
+                   + [[i] for i in range(n_units - ALONE, n_units)])
         couple_of = {}
         recip_slot = {}
-        factor_slot = {}
-        cast_slot = {}
+        scalar_plan = {}
+        vector_end = {}
+        at_slot = 0
         for m, members in enumerate(couples):
-            recip_slot[members[-1] + RECIPROCAL_LAG] = m
-            factor_slot[members[-1] + FACTOR_LAG] = m
+            last = members[-1]
+            recip_slot[last + RECIPROCAL_LAG] = m
             for i in members:
                 couple_of[i] = m
-        at_slot = 0
-        for i in range(n_units):
-            at_slot = max(at_slot + 1, couples[couple_of[i]][-1] + CAST_LAG)
-            cast_slot[at_slot] = i
+            if last >= n_units - ON_VECTOR:
+                vector_end.setdefault(last + FACTOR_LAG, []).append(m)
+                at_slot = max(at_slot, last + FACTOR_LAG)
+                continue
+            scalar_plan.setdefault(max(last + FACTOR_LAG, at_slot), []).append(("factors", m))
+            for i in members:
+                at_slot = max(at_slot + 1, last + CAST_LAG) if len(members) > 1 else max(last + FACTOR_LAG, at_slot)
+                scalar_plan.setdefault(at_slot, []).append(("casts", i))
         n_slots = at_slot + 1
+        last_of = {members[-1]: m for m, members in enumerate(couples)}
+        copies = {}
 
         accs = {}
         prods = {}
@@ -246,35 +262,48 @@ def tile_mha_pa_kernel(tc, x, w, out_0, out_1):
                                         start=(g == 0), stop=(g == PASSES - 1))
             accs[i] = acc
 
+        def half(tile_, i):
+            at = BANK * (i - couples[couple_of[i]][0])
+            return tile_[:, at:at + BANK]
+
         def product_cos(i):
-            t1 = work.tile([P, BANK], F32, tag="t1")
-            t2 = work.tile([P, BANK], F32, tag="t2")
-            prods[i] = (t1, t2)
-            nc.vector.tensor_tensor(out=by_position(t1[:]),
-                                    in0=split(accs[i][:]), in1=split(cos_f), op=ALU.mult)
-
-        def product_sin(i):
-            nc.vector.tensor_tensor(out=by_position(prods[i][1][:]), in0=split(accs[i][:]), in1=split(sin_f), op=ALU.mult)
-
-        def combine(i):
-            t1, t2 = prods[i]
-            osb = outp.tile([P, 2, 2, A], F32, tag="osb")
-            nc.gpsimd.tensor_tensor(out=pairs(osb[:].rearrange("p h s a -> p (h s a)")), in0=pairs(t1[:]), in1=swapped(t2[:]),
-                                    op=ALU.add)
-            results[i] = osb
-
-        def row_max(i):
-            b, c = units[i]
-            osb = results[i]
-            nc.sync.dma_start(out=out_0[b, 2 * c:2 * c + 2].rearrange("h (p s) a -> p h (s a)", s=2),
-                              in_=osb[:].rearrange("p h s a -> p h (s a)"))
             m = couple_of[i]
             if i == couples[m][0]:
-                amax = outp.tile([P, 4 * len(couples[m])], F32, tag="amax")
-                maxima[m] = amax
-            at = 4 * (i - couples[m][0])
-            nc.vector.tensor_reduce(out=maxima[m][:, at:at + 4],
-                                    in_=osb[:].rearrange("p h s a -> p (h s) a"),
+                t1 = work.tile([P, BANK * len(couples[m])], F32, tag="t1")
+                t2 = work.tile([P, BANK * len(couples[m])], F32, tag="t2")
+                prods[m] = (t1, t2)
+            if i in OFFLOAD:
+                ys = banks.tile([P, BANK], F32, tag="ys")
+                nc.scalar.copy(out=ys[:], in_=accs[i][:])
+                copies[i] = ys
+            else:
+                nc.vector.tensor_tensor(out=by_position(half(prods[m][0], i)),
+                                        in0=split(accs[i][:]), in1=split(cos_f), op=ALU.mult)
+
+        def product_cos_late(i):
+            nc.gpsimd.tensor_tensor(out=by_position(half(prods[couple_of[i]][0], i)),
+                                    in0=split(copies[i][:]), in1=split(cos_f), op=ALU.mult)
+
+        def product_sin(i):
+            nc.vector.tensor_tensor(out=by_position(half(prods[couple_of[i]][1], i)), in0=split(accs[i][:]),
+                                    in1=split(sin_f), op=ALU.mult)
+
+        def combine(m):
+            t1, t2 = prods[m]
+            osb = sums.tile([P, len(couples[m]), 2, 2, A], F32, tag="osb")
+            nc.gpsimd.tensor_tensor(out=pairs(osb[:].rearrange("p u h s a -> p (u h s a)")), in0=pairs(t1[:]),
+                                    in1=swapped(t2[:]), op=ALU.add)
+            results[m] = osb
+
+        def row_max(m):
+            osb = results[m]
+            for k, i in enumerate(couples[m]):
+                b, c = units[i]
+                nc.sync.dma_start(out=out_0[b, 2 * c:2 * c + 2].rearrange("h (p s) a -> p h (s a)", s=2),
+                                  in_=osb[:, k].rearrange("p h s a -> p h (s a)"))
+            amax = outp.tile([P, 4 * len(couples[m])], F32, tag="amax")
+            maxima[m] = amax
+            nc.vector.tensor_reduce(out=amax[:], in_=osb[:].rearrange("p u h s a -> p (u h s) a"),
                                     axis=AX.X, op=ALU.max, apply_absolute_value=True)
 
         def reciprocals(m):
@@ -287,18 +316,27 @@ def tile_mha_pa_kernel(tc, x, w, out_0, out_1):
             nc.scalar.activation(out=fac[:], in_=inverses[m][:], func=ACT.Copy, scale=FP8_MAX)
             factors[m] = fac
 
-        def cast_rows(i):
+        def row_factors_on_vector(m):
+            fac = outp.tile([P, 4 * len(couples[m])], F32, tag="fac")
+            nc.vector.tensor_scalar(out=fac[:], in0=inverses[m][:], scalar1=FP8_MAX, scalar2=None, op0=ALU.mult)
+            factors[m] = fac
+
+        def cast_rows(i, on_vector=False):
             b, c = units[i]
-            osb = results[i]
             m = couple_of[i]
+            osb = results[m][:, i - couples[m][0]]
             fac = factors[m]
             at = 4 * (i - couples[m][0])
             o8 = outp.tile([P, 2, 2, A], FP8, tag="o8")
             for hl in range(2):
                 for s in range(2):
                     col = at + 2 * hl + s
-                    nc.scalar.activation(out=o8[:, hl, s, :], in_=osb[:, hl, s, :], func=ACT.Identity,
-                                         scale=fac[:, col:col + 1], bias=zeros[:, 0:1], saturate=False)
+                    if on_vector:
+                        nc.vector.tensor_scalar(out=o8[:, hl, s, :], in0=osb[:, hl, s, :], scalar1=fac[:, col:col + 1],
+                                                scalar2=None, op0=ALU.mult, saturate=False)
+                    else:
+                        nc.scalar.activation(out=o8[:, hl, s, :], in_=osb[:, hl, s, :], func=ACT.Identity,
+                                             scale=fac[:, col:col + 1], bias=zeros[:, 0:1], saturate=False)
             nc.sync.dma_start(out=out_1[b, 2 * c:2 * c + 2].rearrange("h (p s) a -> p h (s a)", s=2),
                               in_=o8[:].bitcast(U8).rearrange("p h s a -> p h (s a)"))
 
@@ -313,14 +351,26 @@ def tile_mha_pa_kernel(tc, x, w, out_0, out_1):
                 product_sin(i - PRODUCT_LAG)
             if quantize_step is not None:
                 quant(quantize_step)
-            if 0 <= i - ROW_MAX_LAG < n_units:
-                row_max(i - ROW_MAX_LAG)
-            if i in cast_slot:
-                cast_rows(cast_slot[i])
-            if i in factor_slot:
-                row_factors(factor_slot[i])
-            if 0 <= i - ADD_LAG < n_units:
-                combine(i - ADD_LAG)
+            if i - ROW_MAX_LAG in last_of:
+                row_max(last_of[i - ROW_MAX_LAG])
+            for m in vector_end.get(i, []):
+                row_factors_on_vector(m)
+                for u in couples[m]:
+                    cast_rows(u, on_vector=True)
+            for what, which in scalar_plan.get(i, []):
+                if what == "factors":
+                    row_factors(which)
+                else:
+                    cast_rows(which)
+            if i - PRODUCT_LAG in OFFLOAD:
+                product_cos_late(i - PRODUCT_LAG)
+            if i - ADD_LAG in last_of:
+                combine(last_of[i - ADD_LAG])
+
+        def quantize_slot(step):
+            first, last = first_of[step], first_of[step + 1] - 1
+            even = [i for i in range(first + QOFF, last + 1) if i % 2 == 0]
+            return even[0] if even else last
 
         with tc.manual_schedule():
             turn(0)
@@ -332,6 +382,6 @@ def tile_mha_pa_kernel(tc, x, w, out_0, out_1):
                 if more:
                     turn(step + 1)
                 for i in range(first_of[step], first_of[step + 1]):
-                    slot(i, step + 1 if more and i == min(first_of[step] + 1, first_of[step + 1] - 1) else None)
+                    slot(i, step + 1 if more and i == quantize_slot(step) else None)
             for i in range(n_units, n_slots):
                 slot(i, None)

@@ -46,7 +46,7 @@ ALONE = 4
 QOFF = 1
 WORK_BUFS = 4
 SUMS_BUFS = 5
-OFFLOAD = ()
+OFFLOAD = (15, 19, 23, 27)
 ON_VECTOR = 1
 
 

@@ -44,6 +44,8 @@ FACTOR_LAG = 5
 CAST_LAG = 6
 ALONE = 4
 QOFF = 1
+SPLIT_FROM = 7
+SPLIT_AFTER = 2
 WORK_BUFS = 4
 SUMS_BUFS = 5
 OFFLOAD = (15, 19, 23, 27)
@@ -166,16 +168,17 @@ def tile_mha_pa_kernel(tc, x, w, out_0, out_1):
         codes = {}
         scales = {}
 
-        def turn(step):
+        def turn(step, halves=(0, 1)):
             kind = STEPS[step][0]
-            grp = grpp.tile([P, STEP_COLUMNS], BF16, tag="grp", align_bytes=64)
-            interleaved[step] = grp
-            gw = grp[:].bitcast(F32)
+            if step not in interleaved:
+                grp = grpp.tile([P, STEP_COLUMNS], BF16, tag="grp", align_bytes=64)
+                interleaved[step] = grp
+            gw = interleaved[step][:].bitcast(F32)
             if kind == "X":
                 view = gw.rearrange("p (j g r u) -> p j g r u", j=2, g=PASSES, u=2)
             else:
                 view = gw.rearrange("p (g j r u) -> p j g r u", g=PASSES, j=2, u=2)
-            for half in range(2):
+            for half in halves:
                 for other in range(2):
                     j, gp = (half, other) if kind == "X" else (other, half)
                     words = raws[step][j][:].bitcast(F32)
@@ -379,9 +382,12 @@ def tile_mha_pa_kernel(tc, x, w, out_0, out_1):
             quant(1)
             for step in range(1, len(STEPS)):
                 more = step + 1 < len(STEPS)
+                split_at = first_of[step] + SPLIT_AFTER if step >= SPLIT_FROM else first_of[step]
                 if more:
-                    turn(step + 1)
+                    turn(step + 1, (0,))
                 for i in range(first_of[step], first_of[step + 1]):
+                    if more and i == split_at:
+                        turn(step + 1, (1,))
                     slot(i, step + 1 if more and i == quantize_slot(step) else None)
             for i in range(n_units, n_slots):
                 slot(i, None)

@@ -94,12 +94,20 @@ def build_tables(nc, const, cos_t, sin_t):
     ang_c = const.tile([P, 2, PAIRS], F32)
     nc.vector.tensor_tensor(out=ang_c[:], in0=shift[:], in1=wrap_c[:], op=ALU.add)
 
+    return ang_s, ang_c
+
+
+def take_sines(nc, const, ang_s, ang_c):
     cos_b = const.tile([P, 2, PAIRS, 2], F32)
     sin_b = const.tile([P, 2, PAIRS, 2], F32)
     nc.scalar.activation(out=sin_b[:, :, :, 0], in_=ang_s[:], func=ACT.Sin, scale=1.0)
     nc.scalar.activation(out=sin_b[:, :, :, 1], in_=ang_s[:], func=ACT.Sin, scale=-1.0)
     nc.scalar.activation(out=cos_b[:, :, :, 0], in_=ang_c[:], func=ACT.Sin, scale=1.0)
     nc.scalar.activation(out=cos_b[:, :, :, 1], in_=ang_c[:], func=ACT.Sin, scale=1.0)
+    return cos_b, sin_b
+
+
+def spread_tables(nc, cos_b, sin_b, cos_t, sin_t):
     for hl in range(2):
         nc.vector.tensor_copy(out=cos_t[:, :, hl, :], in_=cos_b[:].rearrange("p s f e -> p s (f e)"))
         nc.vector.tensor_copy(out=sin_t[:, :, hl, :], in_=sin_b[:].rearrange("p s f e -> p s (f e)"))
@@ -160,7 +168,7 @@ def tile_mha_pa_kernel(tc, x, w, out_0, out_1):
         masks.make_identity(nc, ident[:])
         cos_t = const.tile([P, 2, 2, A], F32)
         sin_t = const.tile([P, 2, 2, A], F32)
-        build_tables(nc, const, cos_t, sin_t)
+        ang_s, ang_c = build_tables(nc, const, cos_t, sin_t)
         cos_f = cos_t[:].rearrange("p s h a -> p (s h a)")
         sin_f = sin_t[:].rearrange("p s h a -> p (s h a)")
 
@@ -378,8 +386,11 @@ def tile_mha_pa_kernel(tc, x, w, out_0, out_1):
         with tc.manual_schedule():
             turn(0)
             quant(0)
-            turn(1)
+            turn(1, (0,))
+            cos_b, sin_b = take_sines(nc, const, ang_s, ang_c)
+            turn(1, (1,))
             quant(1)
+            spread_tables(nc, cos_b, sin_b, cos_t, sin_t)
             for step in range(1, len(STEPS)):
                 more = step + 1 < len(STEPS)
                 split_at = first_of[step] + SPLIT_AFTER if step >= SPLIT_FROM else first_of[step]

@@ -48,7 +48,7 @@ SPLIT_FROM = 7
 SPLIT_AFTER = 2
 WORK_BUFS = 4
 SUMS_BUFS = 5
-OFFLOAD = (15, 19, 23, 27)
+OFFLOAD = (11, 15, 19, 23, 27)
 ON_VECTOR = 1
 
 

@@ -44,6 +44,7 @@ FACTOR_LAG = 5
 CAST_LAG = 6
 ALONE = 4
 QOFF = 1
+COPY_LAG = 0
 SPLIT_FROM = 7
 SPLIT_AFTER = 2
 WORK_BUFS = 4
@@ -283,13 +284,14 @@ def tile_mha_pa_kernel(tc, x, w, out_0, out_1):
                 t1 = work.tile([P, BANK * len(couples[m])], F32, tag="t1")
                 t2 = work.tile([P, BANK * len(couples[m])], F32, tag="t2")
                 prods[m] = (t1, t2)
-            if i in OFFLOAD:
-                ys = banks.tile([P, BANK], F32, tag="ys")
-                nc.scalar.copy(out=ys[:], in_=accs[i][:])
-                copies[i] = ys
-            else:
+            if i not in OFFLOAD:
                 nc.vector.tensor_tensor(out=by_position(half(prods[m][0], i)),
                                         in0=split(accs[i][:]), in1=split(cos_f), op=ALU.mult)
+
+        def copy_bank(i):
+            ys = banks.tile([P, BANK], F32, tag="ys")
+            nc.scalar.copy(out=ys[:], in_=accs[i][:])
+            copies[i] = ys
 
         def product_cos_late(i):
             nc.gpsimd.tensor_tensor(out=by_position(half(prods[couple_of[i]][0], i)),
@@ -373,10 +375,12 @@ def tile_mha_pa_kernel(tc, x, w, out_0, out_1):
                     row_factors(which)
                 else:
                     cast_rows(which)
-            if i - PRODUCT_LAG in OFFLOAD:
-                product_cos_late(i - PRODUCT_LAG)
+            if i - COPY_LAG in OFFLOAD:
+                copy_bank(i - COPY_LAG)
             if i - ADD_LAG in last_of:
                 combine(last_of[i - ADD_LAG])
+            if i - PRODUCT_LAG in OFFLOAD:
+                product_cos_late(i - PRODUCT_LAG)
 
         def quantize_slot(step):
             first, last = first_of[step], first_of[step + 1] - 1

@@ -81,11 +81,19 @@ def build_tables(nc, const, cos_t, sin_t):
     red2 = const.tile([P, 2, PAIRS], F32)
     nc.vector.scalar_tensor_tensor(out=red2[:], in0=turns_f[:], scalar=-TWO_PI_LOW, in1=red1[:],
                                    op0=ALU.mult, op1=ALU.add)
+    return red2
+
+
+def sine_angle(nc, const, red2):
     wrap_s = const.tile([P, 2, PAIRS], F32)
     nc.vector.tensor_scalar(out=wrap_s[:], in0=red2[:], scalar1=math.pi, scalar2=-TWO_PI,
                             op0=ALU.is_gt, op1=ALU.mult)
     ang_s = const.tile([P, 2, PAIRS], F32)
     nc.vector.tensor_tensor(out=ang_s[:], in0=red2[:], in1=wrap_s[:], op=ALU.add)
+    return ang_s
+
+
+def cosine_angle(nc, const, ang_s):
     shift = const.tile([P, 2, PAIRS], F32)
     nc.vector.tensor_scalar(out=shift[:], in0=ang_s[:], scalar1=0.5 * math.pi, scalar2=None,
                             op0=ALU.add)
@@ -94,8 +102,7 @@ def build_tables(nc, const, cos_t, sin_t):
                             op0=ALU.is_gt, op1=ALU.mult)
     ang_c = const.tile([P, 2, PAIRS], F32)
     nc.vector.tensor_tensor(out=ang_c[:], in0=shift[:], in1=wrap_c[:], op=ALU.add)
-
-    return ang_s, ang_c
+    return ang_c
 
 
 def take_sines(nc, const, ang_s, ang_c):
@@ -169,7 +176,7 @@ def tile_mha_pa_kernel(tc, x, w, out_0, out_1):
         masks.make_identity(nc, ident[:])
         cos_t = const.tile([P, 2, 2, A], F32)
         sin_t = const.tile([P, 2, 2, A], F32)
-        ang_s, ang_c = build_tables(nc, const, cos_t, sin_t)
+        red2 = build_tables(nc, const, cos_t, sin_t)
         cos_f = cos_t[:].rearrange("p s h a -> p (s h a)")
         sin_f = sin_t[:].rearrange("p s h a -> p (s h a)")
 
@@ -201,14 +208,16 @@ def tile_mha_pa_kernel(tc, x, w, out_0, out_1):
                     nc.scalar.copy(out=view[:, j, 2 * gp:2 * gp + 2, :, :],
                                    in_=tp[:].rearrange("p g u r -> p g r u"))
 
-        def quant(step):
-            cod = keep.tile([P, STEP_WORDS], U32, tag="cod%d" % step, align_bytes=64)
-            scl = keep.tile([P, STEP_WORDS], U8, tag="scl%d" % step, align_bytes=64)
-            codes[STEPS[step]] = cod
-            scales[STEPS[step]] = scl
+        def quant(step, only=None):
+            if STEPS[step] not in codes:
+                cod = keep.tile([P, STEP_WORDS], U32, tag="cod%d" % step, align_bytes=64)
+                scl = keep.tile([P, STEP_WORDS], U8, tag="scl%d" % step, align_bytes=64)
+                codes[STEPS[step]] = cod
+                scales[STEPS[step]] = scl
+            cod, scl = codes[STEPS[step]], scales[STEPS[step]]
             parts = 2 if step < STEPS_IN_HALVES else 1
             span = STEP_WORDS // parts
-            for part in range(parts):
+            for part in (range(parts) if only is None else (only,)):
                 nc.vector.quantize_mx(out=cod[:, span * part:span * (part + 1)].bitcast(FP8X4),
                                       scales=scl[:, span * part:span * (part + 1)],
                                       in_=interleaved[step][:, 4 * span * part:4 * span * (part + 1)])
@@ -390,11 +399,11 @@ def tile_mha_pa_kernel(tc, x, w, out_0, out_1):
         with tc.manual_schedule():
             turn(0)
             quant(0)
-            turn(1, (0,))
-            cos_b, sin_b = take_sines(nc, const, ang_s, ang_c)
-            turn(1, (1,))
-            quant(1)
-            spread_tables(nc, cos_b, sin_b, cos_t, sin_t)
+            turn(1)
+            quant(1, 0)
+            ang_s = sine_angle(nc, const, red2)
+            quant(1, 1)
+            ang_c = cosine_angle(nc, const, ang_s)
             for step in range(1, len(STEPS)):
                 more = step + 1 < len(STEPS)
                 split_at = first_of[step] + SPLIT_AFTER if step >= SPLIT_FROM else first_of[step]
@@ -403,6 +412,10 @@ def tile_mha_pa_kernel(tc, x, w, out_0, out_1):
                 for i in range(first_of[step], first_of[step + 1]):
                     if more and i == split_at:
                         turn(step + 1, (1,))
+                    if i == 0:
+                        cos_b, sin_b = take_sines(nc, const, ang_s, ang_c)
                     slot(i, step + 1 if more and i == quantize_slot(step) else None)
+                    if i == 0:
+                        spread_tables(nc, cos_b, sin_b, cos_t, sin_t)
             for i in range(n_units, n_slots):
                 slot(i, None)

@@ -53,7 +53,7 @@ OFFLOAD = (11, 15, 19, 23, 27)
 ON_VECTOR = 1
 
 
-def build_tables(nc, const, cos_t, sin_t):
+def build_tables(nc, const):
     pos = const.tile([P, 2], F32)
     nc.gpsimd.iota(pos[:], pattern=[[1, 2]], base=0, channel_multiplier=2,
                    allow_small_or_imprecise_dtypes=True)
@@ -105,36 +105,15 @@ def cosine_angle(nc, const, ang_s):
     return ang_c
 
 
-def take_sines(nc, const, ang_s, ang_c):
-    cos_b = const.tile([P, 2, PAIRS, 2], F32)
-    sin_b = const.tile([P, 2, PAIRS, 2], F32)
-    nc.scalar.activation(out=sin_b[:, :, :, 0], in_=ang_s[:], func=ACT.Sin, scale=1.0)
-    nc.scalar.activation(out=sin_b[:, :, :, 1], in_=ang_s[:], func=ACT.Sin, scale=-1.0)
-    nc.scalar.activation(out=cos_b[:, :, :, 0], in_=ang_c[:], func=ACT.Sin, scale=1.0)
-    nc.scalar.activation(out=cos_b[:, :, :, 1], in_=ang_c[:], func=ACT.Sin, scale=1.0)
-    return cos_b, sin_b
-
-
-def spread_tables(nc, cos_b, sin_b, cos_t, sin_t):
-    for hl in range(2):
-        nc.vector.tensor_copy(out=cos_t[:, :, hl, :], in_=cos_b[:].rearrange("p s f e -> p s (f e)"))
-        nc.vector.tensor_copy(out=sin_t[:, :, hl, :], in_=sin_b[:].rearrange("p s f e -> p s (f e)"))
-
-
-def pairs(ap):
-    return ap.rearrange("p (f e) -> p f e", e=2)
-
-
-def swapped(ap):
-    return pairs(ap)[:, :, ::-1]
+def take_sines(nc, table, ang_s, ang_c):
+    nc.scalar.activation(out=table[:, 0, :, :, 0], in_=ang_c[:], func=ACT.Sin, scale=1.0)
+    nc.scalar.activation(out=table[:, 0, :, :, 1], in_=ang_c[:], func=ACT.Sin, scale=1.0)
+    nc.scalar.activation(out=table[:, 1, :, :, 0], in_=ang_s[:], func=ACT.Sin, scale=1.0)
+    nc.scalar.activation(out=table[:, 1, :, :, 1], in_=ang_s[:], func=ACT.Sin, scale=-1.0)
 
 
 def split(ap):
     return ap.rearrange("p (s h a) -> p s h a", s=2, h=2)
-
-
-def by_position(ap):
-    return ap.rearrange("p (h s a) -> p s h a", s=2, h=2)
 
 
 def tile_mha_pa_kernel(tc, x, w, out_0, out_1):
@@ -174,11 +153,9 @@ def tile_mha_pa_kernel(tc, x, w, out_0, out_1):
         nc.scalar.activation(out=warm[:], in_=zeros[:], func=ACT.Sin)
         ident = const.tile([P, P], F32)
         masks.make_identity(nc, ident[:])
-        cos_t = const.tile([P, 2, 2, A], F32)
-        sin_t = const.tile([P, 2, 2, A], F32)
-        red2 = build_tables(nc, const, cos_t, sin_t)
-        cos_f = cos_t[:].rearrange("p s h a -> p (s h a)")
-        sin_f = sin_t[:].rearrange("p s h a -> p (s h a)")
+        table = const.tile([P, 2, 2, PAIRS, 2], F32)
+        red2 = build_tables(nc, const)
+        both = table[:].rearrange("p t s f e -> p t s (f e)").unsqueeze(3).to_broadcast([P, 2, 2, 2, A])
 
         interleaved = {}
         codes = {}
@@ -283,19 +260,19 @@ def tile_mha_pa_kernel(tc, x, w, out_0, out_1):
                                         start=(g == 0), stop=(g == PASSES - 1))
             accs[i] = acc
 
-        def half(tile_, i):
-            at = BANK * (i - couples[couple_of[i]][0])
-            return tile_[:, at:at + BANK]
-
-        def product_cos(i):
+        def products(i):
             m = couple_of[i]
             if i == couples[m][0]:
-                t1 = work.tile([P, BANK * len(couples[m])], F32, tag="t1")
-                t2 = work.tile([P, BANK * len(couples[m])], F32, tag="t2")
-                prods[m] = (t1, t2)
-            if i not in OFFLOAD:
-                nc.vector.tensor_tensor(out=by_position(half(prods[m][0], i)),
-                                        in0=split(accs[i][:]), in1=split(cos_f), op=ALU.mult)
+                pt = work.tile([P, 2, 2, len(couples[m]), 2, A], F32, tag="pt")
+                prods[m] = pt
+            k = i - couples[m][0]
+            if i in OFFLOAD:
+                nc.vector.tensor_tensor(out=prods[m][:, 1, :, k, :, :], in0=split(accs[i][:]), in1=both[:, 1],
+                                        op=ALU.mult)
+            else:
+                nc.vector.tensor_tensor(out=prods[m][:, :, :, k, :, :],
+                                        in0=split(accs[i][:]).unsqueeze(1).to_broadcast([P, 2, 2, 2, A]),
+                                        in1=both, op=ALU.mult)
 
         def copy_bank(i):
             ys = banks.tile([P, BANK], F32, tag="ys")
@@ -303,18 +280,17 @@ def tile_mha_pa_kernel(tc, x, w, out_0, out_1):
             copies[i] = ys
 
         def product_cos_late(i):
-            nc.gpsimd.tensor_tensor(out=by_position(half(prods[couple_of[i]][0], i)),
-                                    in0=split(copies[i][:]), in1=split(cos_f), op=ALU.mult)
-
-        def product_sin(i):
-            nc.vector.tensor_tensor(out=by_position(half(prods[couple_of[i]][1], i)), in0=split(accs[i][:]),
-                                    in1=split(sin_f), op=ALU.mult)
+            m = couple_of[i]
+            nc.gpsimd.tensor_tensor(out=prods[m][:, 0, :, i - couples[m][0], :, :], in0=split(copies[i][:]),
+                                    in1=both[:, 0], op=ALU.mult)
 
         def combine(m):
-            t1, t2 = prods[m]
+            pt = prods[m]
             osb = sums.tile([P, len(couples[m]), 2, 2, A], F32, tag="osb")
-            nc.gpsimd.tensor_tensor(out=pairs(osb[:].rearrange("p u h s a -> p (u h s a)")), in0=pairs(t1[:]),
-                                    in1=swapped(t2[:]), op=ALU.add)
+            nc.gpsimd.tensor_tensor(out=osb[:].rearrange("p u h s (f e) -> p s (u h) f e", e=2),
+                                    in0=pt[:, 0].rearrange("p s u h (f e) -> p s (u h) f e", e=2),
+                                    in1=pt[:, 1].rearrange("p s u h (f e) -> p s (u h) f e", e=2)[:, :, :, :, ::-1],
+                                    op=ALU.add)
             results[m] = osb
 
         def row_max(m):
@@ -366,13 +342,11 @@ def tile_mha_pa_kernel(tc, x, w, out_0, out_1):
             if i < n_units:
                 multiply(i)
             if 0 <= i - PRODUCT_LAG < n_units:
-                product_cos(i - PRODUCT_LAG)
-            if i in recip_slot:
-                reciprocals(recip_slot[i])
-            if 0 <= i - PRODUCT_LAG < n_units:
-                product_sin(i - PRODUCT_LAG)
+                products(i - PRODUCT_LAG)
             if quantize_step is not None:
                 quant(quantize_step)
+            if i in recip_slot:
+                reciprocals(recip_slot[i])
             if i - ROW_MAX_LAG in last_of:
                 row_max(last_of[i - ROW_MAX_LAG])
             for m in vector_end.get(i, []):
@@ -413,9 +387,7 @@ def tile_mha_pa_kernel(tc, x, w, out_0, out_1):
                     if more and i == split_at:
                         turn(step + 1, (1,))
                     if i == 0:
-                        cos_b, sin_b = take_sines(nc, const, ang_s, ang_c)
+                        take_sines(nc, table, ang_s, ang_c)
                     slot(i, step + 1 if more and i == quantize_slot(step) else None)
-                    if i == 0:
-                        spread_tables(nc, cos_b, sin_b, cos_t, sin_t)
             for i in range(n_units, n_slots):
                 slot(i, None)

@@ -49,7 +49,7 @@ SPLIT_FROM = 7
 SPLIT_AFTER = 2
 WORK_BUFS = 4
 SUMS_BUFS = 5
-OFFLOAD = (11, 15, 19, 23, 27)
+OFFLOAD = (5, 8, 11, 15, 19, 23, 27)
 ON_VECTOR = 1
 
 

import math
from contextlib import ExitStack

import concourse.masks as masks
import concourse.mybir as mybir

F32 = mybir.dt.float32
BF16 = mybir.dt.bfloat16
I32 = mybir.dt.int32
U32 = mybir.dt.uint32
U8 = mybir.dt.uint8
FP8 = mybir.dt.float8_e4m3fn
FP8X4 = mybir.dt.float8_e4m3fn_x4
ALU = mybir.AluOpType
ACT = mybir.ActivationFunctionType
AX = mybir.AxisListType

B, N, W, H, A = 4, 256, 2048, 16, 128
FLOPS = 2 * B * N * W * H * A
P = 128
PASSES = W // (4 * P)
BANK = 512
PAIRS = A // 2
PASS_WORDS = 2 * P
UNIT_HEADS = 2 * A
STEP_COLUMNS = 2 * W
STEP_WORDS = STEP_COLUMNS // 4
FP8_MAX = 448.0

TWO_PI = 2.0 * math.pi
TWO_PI_HIGH = 6.28125
TWO_PI_LOW = TWO_PI - TWO_PI_HIGH
RATIO = 10000.0 ** (-1.0 / (PAIRS - 1))

STEPS = [("W", 0), ("X", 0), ("X", 1), ("W", 1), ("X", 2), ("W", 2), ("X", 3), ("W", 3),
         ("W", 4), ("W", 5), ("W", 6), ("W", 7)]
STEPS_IN_HALVES = 4

PRODUCT_LAG = 1
ADD_LAG = 2
ROW_MAX_LAG = 3
RECIPROCAL_LAG = 4
FACTOR_LAG = 5
CAST_LAG = 6
ALONE = 4
QOFF = 1
COPY_LAG = 0
SPLIT_FROM = 7
SPLIT_AFTER = 2
WORK_BUFS = 4
SUMS_BUFS = 5
OFFLOAD = (5, 8, 11, 15, 19, 23, 27)
ON_VECTOR = 1


def build_tables(nc, const):
    pos = const.tile([P, 2], F32)
    nc.gpsimd.iota(pos[:], pattern=[[1, 2]], base=0, channel_multiplier=2,
                   allow_small_or_imprecise_dtypes=True)
    freq = const.tile([P, PAIRS], F32)
    nc.vector.memset(freq[:, 0:1], 1.0)
    n = 1
    while n < PAIRS:
        nc.vector.tensor_scalar(out=freq[:, n:2 * n], in0=freq[:, 0:n], scalar1=RATIO ** n,
                                scalar2=None, op0=ALU.mult)
        n *= 2
    theta = const.tile([P, 2, PAIRS], F32)
    for s in range(2):
        nc.vector.tensor_scalar(out=theta[:, s, :], in0=freq[:], scalar1=pos[:, s:s + 1],
                                scalar2=None, op0=ALU.mult)
    turns = const.tile([P, 2, PAIRS], F32)
    nc.vector.tensor_scalar(out=turns[:], in0=theta[:], scalar1=1.0 / TWO_PI, scalar2=None,
                            op0=ALU.mult)
    turns_i = const.tile([P, 2, PAIRS], I32)
    nc.vector.tensor_copy(out=turns_i[:], in_=turns[:])
    turns_f = const.tile([P, 2, PAIRS], F32)
    nc.vector.tensor_copy(out=turns_f[:], in_=turns_i[:])
    red1 = const.tile([P, 2, PAIRS], F32)
    nc.vector.scalar_tensor_tensor(out=red1[:], in0=turns_f[:], scalar=-TWO_PI_HIGH, in1=theta[:],
                                   op0=ALU.mult, op1=ALU.add)
    red2 = const.tile([P, 2, PAIRS], F32)
    nc.vector.scalar_tensor_tensor(out=red2[:], in0=turns_f[:], scalar=-TWO_PI_LOW, in1=red1[:],
                                   op0=ALU.mult, op1=ALU.add)
    return red2


def sine_angle(nc, const, red2):
    wrap_s = const.tile([P, 2, PAIRS], F32)
    nc.vector.tensor_scalar(out=wrap_s[:], in0=red2[:], scalar1=math.pi, scalar2=-TWO_PI,
                            op0=ALU.is_gt, op1=ALU.mult)
    ang_s = const.tile([P, 2, PAIRS], F32)
    nc.vector.tensor_tensor(out=ang_s[:], in0=red2[:], in1=wrap_s[:], op=ALU.add)
    return ang_s


def cosine_angle(nc, const, ang_s):
    shift = const.tile([P, 2, PAIRS], F32)
    nc.vector.tensor_scalar(out=shift[:], in0=ang_s[:], scalar1=0.5 * math.pi, scalar2=None,
                            op0=ALU.add)
    wrap_c = const.tile([P, 2, PAIRS], F32)
    nc.vector.tensor_scalar(out=wrap_c[:], in0=shift[:], scalar1=math.pi, scalar2=-TWO_PI,
                            op0=ALU.is_gt, op1=ALU.mult)
    ang_c = const.tile([P, 2, PAIRS], F32)
    nc.vector.tensor_tensor(out=ang_c[:], in0=shift[:], in1=wrap_c[:], op=ALU.add)
    return ang_c


def take_sines(nc, table, ang_s, ang_c):
    nc.scalar.activation(out=table[:, 0, :, :, 0], in_=ang_c[:], func=ACT.Sin, scale=1.0)
    nc.scalar.activation(out=table[:, 0, :, :, 1], in_=ang_c[:], func=ACT.Sin, scale=1.0)
    nc.scalar.activation(out=table[:, 1, :, :, 0], in_=ang_s[:], func=ACT.Sin, scale=1.0)
    nc.scalar.activation(out=table[:, 1, :, :, 1], in_=ang_s[:], func=ACT.Sin, scale=-1.0)


def split(ap):
    return ap.rearrange("p (s h a) -> p s h a", s=2, h=2)


def tile_mha_pa_kernel(tc, x, w, out_0, out_1):
    nc = tc.nc
    with ExitStack() as ctx:
        const = ctx.enter_context(tc.tile_pool(name="const", bufs=1))
        rawp = ctx.enter_context(tc.tile_pool(name="raw", bufs=16))
        grpp = ctx.enter_context(tc.tile_pool(name="grp", bufs=3))
        keep = ctx.enter_context(tc.tile_pool(name="keep", bufs=1))
        work = ctx.enter_context(tc.tile_pool(name="work", bufs=WORK_BUFS))
        sums = ctx.enter_context(tc.tile_pool(name="sums", bufs=SUMS_BUFS))
        banks = ctx.enter_context(tc.tile_pool(name="banks", bufs=2))
        outp = ctx.enter_context(tc.tile_pool(name="outp", bufs=9))
        tpp = ctx.enter_context(tc.psum_pool(name="tpp", bufs=4))
        accp = ctx.enter_context(tc.psum_pool(name="accp", bufs=4))

        raws = []
        for kind, which in STEPS:
            tiles = []
            for j in range(2):
                raw = rawp.tile([P, W], BF16, tag="raw")
                if kind == "X":
                    src = x[which].rearrange("(p s) k -> p s k", s=2)[:, j, :]
                else:
                    src = w[(2 * which + j) * P:(2 * which + j + 1) * P, :]
                pieces = 2 if len(raws) < STEPS_IN_HALVES else 1
                wide = W // pieces
                for piece in range(pieces):
                    nc.sync.dma_start(out=raw[:, piece * wide:(piece + 1) * wide],
                                      in_=src[:, piece * wide:(piece + 1) * wide])
                tiles.append(raw)
            raws.append(tiles)

        zeros = const.tile([P, 1], F32)
        nc.vector.memset(zeros[:], 0.0)
        warm = const.tile([P, 1], F32)
        nc.scalar.activation(out=warm[:], in_=zeros[:], func=ACT.Sin)
        ident = const.tile([P, P], F32)
        masks.make_identity(nc, ident[:])
        table = const.tile([P, 2, 2, PAIRS, 2], F32)
        red2 = build_tables(nc, const)
        both = table[:].rearrange("p t s f e -> p t s (f e)").unsqueeze(3).to_broadcast([P, 2, 2, 2, A])

        interleaved = {}
        codes = {}
        scales = {}

        def turn(step, halves=(0, 1)):
            kind = STEPS[step][0]
            if step not in interleaved:
                grp = grpp.tile([P, STEP_COLUMNS], BF16, tag="grp", align_bytes=64)
                interleaved[step] = grp
            gw = interleaved[step][:].bitcast(F32)
            if kind == "X":
                view = gw.rearrange("p (j g r u) -> p j g r u", j=2, g=PASSES, u=2)
            else:
                view = gw.rearrange("p (g j r u) -> p j g r u", g=PASSES, j=2, u=2)
            for half in halves:
                for other in range(2):
                    j, gp = (half, other) if kind == "X" else (other, half)
                    words = raws[step][j][:].bitcast(F32)
                    tp = tpp.tile([P, 2, 2, P], F32, tag="tp")
                    for gg in range(2):
                        g = 2 * gp + gg
                        for u in range(2):
                            nc.tensor.transpose(out=tp[:, gg, u, :],
                                                in_=words[:, PASS_WORDS * g + u:PASS_WORDS * (g + 1):2],
                                                identity=ident[:])
                    nc.scalar.copy(out=view[:, j, 2 * gp:2 * gp + 2, :, :],
                                   in_=tp[:].rearrange("p g u r -> p g r u"))

        def quant(step, only=None):
            if STEPS[step] not in codes:
                cod = keep.tile([P, STEP_WORDS], U32, tag="cod%d" % step, align_bytes=64)
                scl = keep.tile([P, STEP_WORDS], U8, tag="scl%d" % step, align_bytes=64)
                codes[STEPS[step]] = cod
                scales[STEPS[step]] = scl
            cod, scl = codes[STEPS[step]], scales[STEPS[step]]
            parts = 2 if step < STEPS_IN_HALVES else 1
            span = STEP_WORDS // parts
            for part in (range(parts) if only is None else (only,)):
                nc.vector.quantize_mx(out=cod[:, span * part:span * (part + 1)].bitcast(FP8X4),
                                      scales=scl[:, span * part:span * (part + 1)],
                                      in_=interleaved[step][:, 4 * span * part:4 * span * (part + 1)])

        units = []
        first_of = []
        have = {"X": [], "W": []}
        for kind, which in STEPS:
            first_of.append(len(units))
            if kind == "X":
                units.extend([(which, c) for c in have["W"]])
            else:
                units.extend([(b, which) for b in have["X"]])
            have[kind].append(which)
        first_of.append(len(units))
        n_units = len(units)

        couples = ([[2 * m, 2 * m + 1] for m in range((n_units - ALONE) // 2)]
                   + [[i] for i in range(n_units - ALONE, n_units)])
        couple_of = {}
        recip_slot = {}
        scalar_plan = {}
        vector_end = {}
        at_slot = 0
        for m, members in enumerate(couples):
            last = members[-1]
            recip_slot[last + RECIPROCAL_LAG] = m
            for i in members:
                couple_of[i] = m
            if last >= n_units - ON_VECTOR:
                vector_end.setdefault(last + FACTOR_LAG, []).append(m)
                at_slot = max(at_slot, last + FACTOR_LAG)
                continue
            scalar_plan.setdefault(max(last + FACTOR_LAG, at_slot), []).append(("factors", m))
            for i in members:
                at_slot = max(at_slot + 1, last + CAST_LAG) if len(members) > 1 else max(last + FACTOR_LAG, at_slot)
                scalar_plan.setdefault(at_slot, []).append(("casts", i))
        n_slots = at_slot + 1
        last_of = {members[-1]: m for m, members in enumerate(couples)}
        copies = {}

        accs = {}
        prods = {}
        results = {}
        maxima = {}
        inverses = {}
        factors = {}

        def multiply(i):
            b, c = units[i]
            xc, xs = codes[("X", b)], scales[("X", b)]
            wc, ws = codes[("W", c)], scales[("W", c)]
            acc = accp.tile([P, BANK], F32, tag="acc")
            for s in range(2):
                for g in range(PASSES):
                    xo = (PASSES * s + g) * P
                    wo = g * UNIT_HEADS
                    nc.tensor.matmul_mx(out=acc[:, UNIT_HEADS * s:UNIT_HEADS * (s + 1)],
                                        lhsT=xc[:, xo:xo + P].bitcast(FP8X4),
                                        lhsT_scale=xs[:, xo:xo + P],
                                        rhs=wc[:, wo:wo + UNIT_HEADS].bitcast(FP8X4),
                                        rhs_scale=ws[:, wo:wo + UNIT_HEADS],
                                        start=(g == 0), stop=(g == PASSES - 1))
            accs[i] = acc

        def products(i):
            m = couple_of[i]
            if i == couples[m][0]:
                pt = work.tile([P, 2, 2, len(couples[m]), 2, A], F32, tag="pt")
                prods[m] = pt
            k = i - couples[m][0]
            if i in OFFLOAD:
                nc.vector.tensor_tensor(out=prods[m][:, 1, :, k, :, :], in0=split(accs[i][:]), in1=both[:, 1],
                                        op=ALU.mult)
            else:
                nc.vector.tensor_tensor(out=prods[m][:, :, :, k, :, :],
                                        in0=split(accs[i][:]).unsqueeze(1).to_broadcast([P, 2, 2, 2, A]),
                                        in1=both, op=ALU.mult)

        def copy_bank(i):
            ys = banks.tile([P, BANK], F32, tag="ys")
            nc.scalar.copy(out=ys[:], in_=accs[i][:])
            copies[i] = ys

        def product_cos_late(i):
            m = couple_of[i]
            nc.gpsimd.tensor_tensor(out=prods[m][:, 0, :, i - couples[m][0], :, :], in0=split(copies[i][:]),
                                    in1=both[:, 0], op=ALU.mult)

        def combine(m):
            pt = prods[m]
            osb = sums.tile([P, len(couples[m]), 2, 2, A], F32, tag="osb")
            nc.gpsimd.tensor_tensor(out=osb[:].rearrange("p u h s (f e) -> p s (u h) f e", e=2),
                                    in0=pt[:, 0].rearrange("p s u h (f e) -> p s (u h) f e", e=2),
                                    in1=pt[:, 1].rearrange("p s u h (f e) -> p s (u h) f e", e=2)[:, :, :, :, ::-1],
                                    op=ALU.add)
            results[m] = osb

        def row_max(m):
            osb = results[m]
            for k, i in enumerate(couples[m]):
                b, c = units[i]
                nc.sync.dma_start(out=out_0[b, 2 * c:2 * c + 2].rearrange("h (p s) a -> p h (s a)", s=2),
                                  in_=osb[:, k].rearrange("p h s a -> p h (s a)"))
            amax = outp.tile([P, 4 * len(couples[m])], F32, tag="amax")
            maxima[m] = amax
            nc.vector.tensor_reduce(out=amax[:], in_=osb[:].rearrange("p u h s a -> p (u h s) a"),
                                    axis=AX.X, op=ALU.max, apply_absolute_value=True)

        def reciprocals(m):
            rinv = outp.tile([P, 4 * len(couples[m])], F32, tag="rinv")
            nc.vector.reciprocal(out=rinv[:], in_=maxima[m][:])
            inverses[m] = rinv

        def row_factors(m):
            fac = outp.tile([P, 4 * len(couples[m])], F32, tag="fac")
            nc.scalar.activation(out=fac[:], in_=inverses[m][:], func=ACT.Copy, scale=FP8_MAX)
            factors[m] = fac

        def row_factors_on_vector(m):
            fac = outp.tile([P, 4 * len(couples[m])], F32, tag="fac")
            nc.vector.tensor_scalar(out=fac[:], in0=inverses[m][:], scalar1=FP8_MAX, scalar2=None, op0=ALU.mult)
            factors[m] = fac

        def cast_rows(i, on_vector=False):
            b, c = units[i]
            m = couple_of[i]
            osb = results[m][:, i - couples[m][0]]
            fac = factors[m]
            at = 4 * (i - couples[m][0])
            o8 = outp.tile([P, 2, 2, A], FP8, tag="o8")
            for hl in range(2):
                for s in range(2):
                    col = at + 2 * hl + s
                    if on_vector:
                        nc.vector.tensor_scalar(out=o8[:, hl, s, :], in0=osb[:, hl, s, :], scalar1=fac[:, col:col + 1],
                                                scalar2=None, op0=ALU.mult, saturate=False)
                    else:
                        nc.scalar.activation(out=o8[:, hl, s, :], in_=osb[:, hl, s, :], func=ACT.Identity,
                                             scale=fac[:, col:col + 1], bias=zeros[:, 0:1], saturate=False)
            nc.sync.dma_start(out=out_1[b, 2 * c:2 * c + 2].rearrange("h (p s) a -> p h (s a)", s=2),
                              in_=o8[:].bitcast(U8).rearrange("p h s a -> p h (s a)"))

        def slot(i, quantize_step):
            if i < n_units:
                multiply(i)
            if 0 <= i - PRODUCT_LAG < n_units:
                products(i - PRODUCT_LAG)
            if quantize_step is not None:
                quant(quantize_step)
            if i in recip_slot:
                reciprocals(recip_slot[i])
            if i - ROW_MAX_LAG in last_of:
                row_max(last_of[i - ROW_MAX_LAG])
            for m in vector_end.get(i, []):
                row_factors_on_vector(m)
                for u in couples[m]:
                    cast_rows(u, on_vector=True)
            for what, which in scalar_plan.get(i, []):
                if what == "factors":
                    row_factors(which)
                else:
                    cast_rows(which)
            if i - COPY_LAG in OFFLOAD:
                copy_bank(i - COPY_LAG)
            if i - ADD_LAG in last_of:
                combine(last_of[i - ADD_LAG])
            if i - PRODUCT_LAG in OFFLOAD:
                product_cos_late(i - PRODUCT_LAG)

        def quantize_slot(step):
            first, last = first_of[step], first_of[step + 1] - 1
            even = [i for i in range(first + QOFF, last + 1) if i % 2 == 0]
            return even[0] if even else last

        with tc.manual_schedule():
            turn(0)
            quant(0)
            turn(1)
            quant(1, 0)
            ang_s = sine_angle(nc, const, red2)
            quant(1, 1)
            ang_c = cosine_angle(nc, const, ang_s)
            for step in range(1, len(STEPS)):
                more = step + 1 < len(STEPS)
                split_at = first_of[step] + SPLIT_AFTER if step >= SPLIT_FROM else first_of[step]
                if more:
                    turn(step + 1, (0,))
                for i in range(first_of[step], first_of[step + 1]):
                    if more and i == split_at:
                        turn(step + 1, (1,))
                    if i == 0:
                        take_sines(nc, table, ang_s, ang_c)
                    slot(i, step + 1 if more and i == quantize_slot(step) else None)
            for i in range(n_units, n_slots):
                slot(i, None)
